import numpy as np
import ml_dtypes


def mxq(x, axis, fmt="e4m3"):
    dtype, down = {"e4m3": (ml_dtypes.float8_e4m3fn, 7), "e5m2": (ml_dtypes.float8_e5m2, 14)}[fmt]
    v = np.moveaxis(np.asarray(x, np.float32).astype(ml_dtypes.bfloat16).astype(np.float64), axis, -1)
    blocks = v.reshape(v.shape[:-1] + (-1, 32))
    amax = np.abs(blocks).max(-1, keepdims=True)
    byte = np.maximum(np.where(amax > 0, np.frexp(amax)[1] - 1 + 127, 0) - down, 1)
    scale = np.exp2(byte - 127.0)
    codes = (blocks / scale).astype(np.float32).astype(dtype).astype(np.float64)
    return np.moveaxis((codes * scale).reshape(v.shape), -1, axis)


WIDE = False


def mx_kscale(k):
    if not WIDE:
        return np.ones(k)
    levels = np.array([10, -10, 5, -5, 0])
    a = np.random.permutation(np.resize(levels, k // 512 * 4)).reshape(k // 512, 4)
    idx = np.arange(k)
    return np.exp2(a[idx // 512, idx % 128 // 32])


BF16 = ml_dtypes.bfloat16


def bf(x):
    return np.asarray(x, np.float32).astype(BF16)


def f64(x):
    return np.asarray(x).astype(np.float64)


B, T, D, E, H, L = 128, 41, 1024, 128, 128, 1
TM = T - L
F = H + L * D + 1


def setup_inputs():
    s = mx_kscale(D)
    we = np.random.standard_normal((D, H)) / np.sqrt(H)
    wy = np.random.standard_normal((D, L, D)) * 0.7 / np.sqrt(L * D) / s
    wx = np.random.standard_normal((D, 1)) * 0.5 / s[:, None]
    return {"x": bf(np.random.standard_normal((B, T, D)) * s),
            "emb": bf(np.random.standard_normal((B, H)) * 0.5),
            "Wg": bf(np.concatenate([we, wy.reshape(D, L * D), wx], axis=1)),
            "bg": bf(np.random.standard_normal(D) * 0.3)}


def reference(x, emb, Wg, bg):
    xf = f64(x)
    Wy = f64(Wg)[:, H:H + L * D].reshape(D, L, D)
    wx = f64(Wg)[:, -1]
    ctx = f64(emb) @ f64(Wg)[:, :H].T
    xq = mxq(xf[:, :T - 1, :], 2, "e4m3")
    wq = mxq(Wy, 2, "e4m3")
    lag = sum((xq[:, l:TM + l, :] @ wq[:, l, :].T) for l in range(L))
    return ctx[:, None, :] + lag + xf[:, L:, :] * wx + f64(bg)

@@ -1,0 +1,198 @@
+from contextlib import ExitStack
+
+import concourse.mybir as mybir
+from concourse.masks import make_identity
+
+F32 = mybir.dt.float32
+BF16 = mybir.dt.bfloat16
+U32 = mybir.dt.uint32
+U8 = mybir.dt.uint8
+FP8X4 = mybir.dt.float8_e4m3fn_x4
+ADD = mybir.AluOpType.add
+MULT = mybir.AluOpType.mult
+
+P = 128
+STEPS = 41
+LAGS = STEPS - 1
+D = 1024
+ROW = P + D + 1
+ROW_PAD = 1168
+PASSES = 2
+WORD_BLOCKS = 4
+SLABS = 8
+CHUNK = 4
+N_CHUNKS = LAGS // CHUNK
+BANK = 512
+
+FLOPS = 2 * P * LAGS * D * D + 2 * P * P * D
+
+
+def regroup(copy, bank, grouped):
+    halves = bank.bitcast(BF16).rearrange("p (g u) (c e) -> p g c u e", u=2, e=2)
+    for g in range(PASSES):
+        copy(out=grouped[:, g].rearrange("p c (u e) -> p c u e", e=2), in_=halves[:, g])
+
+
+def tile_npchangetransitionprior_pa_t_kernel(tc, x, emb, Wg, bg, out):
+    nc = tc.nc
+    with ExitStack() as ctx:
+        const = ctx.enter_context(tc.tile_pool(name="const", bufs=1))
+        xs_pool = ctx.enter_context(tc.tile_pool(name="xs_pool", bufs=3))
+        xg_pool = ctx.enter_context(tc.tile_pool(name="xg_pool", bufs=3))
+        xq_pool = ctx.enter_context(tc.tile_pool(name="xq_pool", bufs=2))
+        sum_pool = ctx.enter_context(tc.tile_pool(name="sum_pool", bufs=2))
+        res_pool = ctx.enter_context(tc.tile_pool(name="res_pool", bufs=2))
+        psum_in = ctx.enter_context(tc.psum_pool(name="psum_in", bufs=2))
+        psum_mx = ctx.enter_context(tc.psum_pool(name="psum_mx", bufs=3))
+        psum_back = ctx.enter_context(tc.psum_pool(name="psum_back", bufs=3))
+
+        x_rows = {}
+        x_grouped = {}
+        x_codes = {}
+        x_scales = {}
+
+        def load_chunk(c):
+            n_steps = min(CHUNK, STEPS - CHUNK * c)
+            rows = xs_pool.tile([P, CHUNK, D], BF16, name="rows")
+            nc.sync.dma_start(out=rows[:, 0:n_steps, :], in_=x[:, CHUNK * c : CHUNK * c + n_steps, :])
+            x_rows[c] = rows
+
+        load_chunk(0)
+        wg = const.tile([P, WORD_BLOCKS, 2, ROW_PAD], BF16, name="wg")
+        wg_rows = Wg.rearrange("(w p e) c -> w p e c", p=P, e=2)
+        for w in range(WORD_BLOCKS):
+            nc.sync.dma_start(out=wg[:, w, :, 0:ROW], in_=wg_rows[w])
+        load_chunk(1)
+        load_chunk(2)
+        emb_rows = const.tile([P, P], BF16, name="emb_rows")
+        nc.scalar.dma_start(out=emb_rows[:], in_=emb)
+        bias_row = const.tile([P, D], BF16, name="bias_row")
+        nc.vector.memset(bias_row[:], 0.0)
+        nc.scalar.dma_start(out=bias_row[0:1, :], in_=bg.rearrange("(o d) -> o d", o=1))
+        ones = const.tile([P, P], BF16, name="ones")
+        nc.vector.memset(ones[:], 1.0)
+        ident_f32 = const.tile([P, P], F32, name="ident_f32")
+        make_identity(nc, ident_f32[:])
+        ident_bf16 = const.tile([P, P], BF16, name="ident_bf16")
+        make_identity(nc, ident_bf16[:])
+
+        def transpose_step(c, s):
+            words = x_rows[c][:].bitcast(F32)
+            bank = psum_in.tile([P, WORD_BLOCKS, P], F32, name="bank_in")
+            for w in range(WORD_BLOCKS):
+                nc.tensor.transpose(bank[:, w, :], words[:, s, P * w : P * (w + 1)], ident_f32[:])
+            if c < N_CHUNKS:
+                if s == 0:
+                    x_grouped[c] = xg_pool.tile([P, PASSES, CHUNK + 1, P, 4], BF16, name="grouped", align_bytes=64)
+                regroup(nc.scalar.copy, bank[:], x_grouped[c][:, :, s, :, :])
+            if s == 0 and c > 0:
+                regroup(nc.scalar.copy, bank[:], x_grouped[c - 1][:, :, CHUNK, :, :])
+
+        def quantise_chunk(c):
+            codes = xq_pool.tile([P, PASSES, BANK], U32, name="codes", align_bytes=64)
+            scales = xq_pool.tile([P, PASSES, BANK], U8, name="scales", align_bytes=64)
+            for g in range(PASSES):
+                nc.vector.quantize_mx(
+                    out=codes[:, g, :].bitcast(FP8X4),
+                    scales=scales[:, g, :],
+                    in_=x_grouped[c][:, g, 0:CHUNK, :, :].rearrange("p s b v -> p (s b v)"),
+                )
+            x_codes[c] = codes
+            x_scales[c] = scales
+
+        for s in range(CHUNK):
+            transpose_step(0, s)
+
+        wg_words = wg[:].bitcast(F32)
+        wy_word0 = P // 2
+        wy_grouped = const.tile([P, SLABS, PASSES, P, 4], BF16, name="wy_grouped", align_bytes=64)
+        wy_codes = const.tile([P, SLABS, PASSES, P], U32, name="wy_codes", align_bytes=64)
+        wy_scales = const.tile([P, SLABS, PASSES, P], U8, name="wy_scales", align_bytes=64)
+        for w in range(WORD_BLOCKS):
+            for e in range(2):
+                bank = psum_in.tile([P, WORD_BLOCKS, P], F32, name="bank_in")
+                for k in range(WORD_BLOCKS):
+                    first = wy_word0 + P * k
+                    nc.tensor.transpose(bank[:, k, :], wg_words[:, w, e, first : first + P], ident_f32[:])
+                copy = nc.vector.tensor_copy if e == 0 else nc.scalar.copy
+                regroup(copy, bank[:], wy_grouped[:, 2 * w + e])
+            nc.vector.quantize_mx(
+                out=wy_codes[:, 2 * w : 2 * w + 2].rearrange("p l g m -> p (l g m)").bitcast(FP8X4),
+                scales=wy_scales[:, 2 * w : 2 * w + 2].rearrange("p l g m -> p (l g m)"),
+                in_=wy_grouped[:, 2 * w : 2 * w + 2].rearrange("p l g m v -> p (l g m v)"),
+            )
+        wx = const.tile([P, SLABS], F32, name="wx")
+        nc.vector.tensor_copy(out=wx[:].rearrange("p (w e) -> p w e", e=2), in_=wg[:, :, :, ROW - 1])
+
+        for s in range(CHUNK):
+            transpose_step(1, s)
+        quantise_chunk(0)
+
+        emb_t_ps = psum_back.tile([P, P], BF16, name="emb_t_ps", tag="bank_back")
+        nc.tensor.transpose(emb_t_ps[:], emb_rows[:], ident_bf16[:])
+        emb_t = const.tile([P, P], BF16, name="emb_t")
+        nc.scalar.copy(out=emb_t[:], in_=emb_t_ps[:])
+        we_t_ps = psum_back.tile([P, SLABS, P], BF16, name="we_t_ps", tag="bank_back")
+        for w in range(WORD_BLOCKS):
+            for e in range(2):
+                nc.tensor.transpose(we_t_ps[:, 2 * w + e, :], wg[:, w, e, 0:P], ident_bf16[:])
+        we_t = const.tile([P, D], BF16, name="we_t")
+        nc.scalar.copy(
+            out=we_t[:].rearrange("h (w p e) -> h w p e", p=P, e=2),
+            in_=we_t_ps[:].rearrange("h (w e) p -> h w p e", e=2),
+        )
+        context = const.tile([P, D], F32, name="context")
+        for n in range(D // BANK):
+            cols = slice(BANK * n, BANK * (n + 1))
+            context_ps = psum_mx.tile([P, BANK], F32, name="context_ps", tag="product")
+            nc.tensor.matmul(context_ps[:], lhsT=emb_t[:], rhs=we_t[:, cols], start=True, stop=False)
+            nc.tensor.matmul(context_ps[:], lhsT=ones[:], rhs=bias_row[:, cols], start=False, stop=True)
+            nc.scalar.copy(out=context[:, cols], in_=context_ps[:])
+
+        for i in range(N_CHUNKS):
+            if CHUNK * (i + 3) < STEPS:
+                load_chunk(i + 3)
+
+            sums = sum_pool.tile([P, SLABS, BANK], F32, name="sums")
+            for slab in range(SLABS):
+                product = psum_mx.tile([P, BANK], F32, name="product")
+                for g in range(PASSES):
+                    nc.tensor.matmul_mx(
+                        out=product[:],
+                        lhsT=wy_codes[:, slab, g, :].bitcast(FP8X4),
+                        lhsT_scale=wy_scales[:, slab, g, :],
+                        rhs=x_codes[i][:, g, :].bitcast(FP8X4),
+                        rhs_scale=x_scales[i][:, g, :],
+                        start=(g == 0),
+                        stop=(g == PASSES - 1),
+                    )
+                nc.vector.scalar_tensor_tensor(
+                    out=sums[:, slab, :].rearrange("p (s b) -> p s b", s=CHUNK),
+                    in0=x_grouped[i][:, slab // 4, 1 : CHUNK + 1, :, slab % 4],
+                    scalar=wx[:, slab : slab + 1],
+                    in1=product[:].rearrange("p (s b) -> p s b", s=CHUNK),
+                    op0=MULT,
+                    op1=ADD,
+                )
+
+            if i + 1 < N_CHUNKS:
+                quantise_chunk(i + 1)
+
+            res = res_pool.tile([P, CHUNK, D], F32, name="res")
+            for n in range(D // BANK):
+                cols = slice(BANK * n, BANK * (n + 1))
+                for s in range(CHUNK):
+                    bank = psum_back.tile([P, 4, P], F32, name="bank_back")
+                    for q in range(4):
+                        nc.tensor.transpose(bank[:, q, :], sums[:, 4 * n + q, P * s : P * (s + 1)], ident_f32[:])
+                    nc.vector.tensor_tensor(
+                        out=res[:, s, cols].rearrange("b (u p e) -> b u p e", u=2, e=2),
+                        in0=bank[:].rearrange("b (u e) p -> b u p e", e=2),
+                        in1=context[:, cols].rearrange("b (u p e) -> b u p e", u=2, e=2),
+                        op=ADD,
+                    )
+                    if s % 2 == 1:
+                        step = 2 * n + s // 2
+                        if CHUNK * (i + 2) + step < STEPS:
+                            transpose_step(i + 2, step)
+            nc.sync.dma_start(out=out[:, CHUNK * i : CHUNK * (i + 1), :], in_=res[:])

@@ -36,12 +36,13 @@ def regroup(copy, bank, grouped):
 def tile_npchangetransitionprior_pa_t_kernel(tc, x, emb, Wg, bg, out):
     nc = tc.nc
     with ExitStack() as ctx:
+        ctx.enter_context(tc.manual_schedule())
         const = ctx.enter_context(tc.tile_pool(name="const", bufs=1))
         xs_pool = ctx.enter_context(tc.tile_pool(name="xs_pool", bufs=3))
         xg_pool = ctx.enter_context(tc.tile_pool(name="xg_pool", bufs=3))
         xq_pool = ctx.enter_context(tc.tile_pool(name="xq_pool", bufs=2))
         sum_pool = ctx.enter_context(tc.tile_pool(name="sum_pool", bufs=2))
-        res_pool = ctx.enter_context(tc.tile_pool(name="res_pool", bufs=2))
+        res_pool = ctx.enter_context(tc.tile_pool(name="res_pool", bufs=4))
         psum_in = ctx.enter_context(tc.psum_pool(name="psum_in", bufs=2))
         psum_mx = ctx.enter_context(tc.psum_pool(name="psum_mx", bufs=3))
         psum_back = ctx.enter_context(tc.psum_pool(name="psum_back", bufs=3))
@@ -50,6 +51,7 @@ def tile_npchangetransitionprior_pa_t_kernel(tc, x, emb, Wg, bg, out):
         x_grouped = {}
         x_codes = {}
         x_scales = {}
+        sums = {}
 
         def load_chunk(c):
             n_steps = min(CHUNK, STEPS - CHUNK * c)
@@ -88,17 +90,15 @@ def tile_npchangetransitionprior_pa_t_kernel(tc, x, emb, Wg, bg, out):
             if s == 0 and c > 0:
                 regroup(nc.scalar.copy, bank[:], x_grouped[c - 1][:, :, CHUNK, :, :])
 
-        def quantise_chunk(c):
-            codes = xq_pool.tile([P, PASSES, BANK], U32, name="codes", align_bytes=64)
-            scales = xq_pool.tile([P, PASSES, BANK], U8, name="scales", align_bytes=64)
-            for g in range(PASSES):
-                nc.vector.quantize_mx(
-                    out=codes[:, g, :].bitcast(FP8X4),
-                    scales=scales[:, g, :],
-                    in_=x_grouped[c][:, g, 0:CHUNK, :, :].rearrange("p s b v -> p (s b v)"),
-                )
-            x_codes[c] = codes
-            x_scales[c] = scales
+        def quantise_pass(c, g):
+            if g == 0:
+                x_codes[c] = xq_pool.tile([P, PASSES, BANK], U32, name="codes", align_bytes=64)
+                x_scales[c] = xq_pool.tile([P, PASSES, BANK], U8, name="scales", align_bytes=64)
+            nc.vector.quantize_mx(
+                out=x_codes[c][:, g, :].bitcast(FP8X4),
+                scales=x_scales[c][:, g, :],
+                in_=x_grouped[c][:, g, 0:CHUNK, :, :].rearrange("p s b v -> p (s b v)"),
+            )
 
         for s in range(CHUNK):
             transpose_step(0, s)
@@ -126,7 +126,8 @@ def tile_npchangetransitionprior_pa_t_kernel(tc, x, emb, Wg, bg, out):
 
         for s in range(CHUNK):
             transpose_step(1, s)
-        quantise_chunk(0)
+        for g in range(PASSES):
+            quantise_pass(0, g)
 
         emb_t_ps = psum_back.tile([P, P], BF16, name="emb_t_ps", tag="bank_back")
         nc.tensor.transpose(emb_t_ps[:], emb_rows[:], ident_bf16[:])
@@ -149,50 +150,54 @@ def tile_npchangetransitionprior_pa_t_kernel(tc, x, emb, Wg, bg, out):
             nc.tensor.matmul(context_ps[:], lhsT=ones[:], rhs=bias_row[:, cols], start=False, stop=True)
             nc.scalar.copy(out=context[:, cols], in_=context_ps[:])
 
-        for i in range(N_CHUNKS):
-            if CHUNK * (i + 3) < STEPS:
-                load_chunk(i + 3)
-
-            sums = sum_pool.tile([P, SLABS, BANK], F32, name="sums")
-            for slab in range(SLABS):
-                product = psum_mx.tile([P, BANK], F32, name="product")
-                for g in range(PASSES):
-                    nc.tensor.matmul_mx(
-                        out=product[:],
-                        lhsT=wy_codes[:, slab, g, :].bitcast(FP8X4),
-                        lhsT_scale=wy_scales[:, slab, g, :],
-                        rhs=x_codes[i][:, g, :].bitcast(FP8X4),
-                        rhs_scale=x_scales[i][:, g, :],
-                        start=(g == 0),
-                        stop=(g == PASSES - 1),
-                    )
-                nc.vector.scalar_tensor_tensor(
-                    out=sums[:, slab, :].rearrange("p (s b) -> p s b", s=CHUNK),
-                    in0=x_grouped[i][:, slab // 4, 1 : CHUNK + 1, :, slab % 4],
-                    scalar=wx[:, slab : slab + 1],
-                    in1=product[:].rearrange("p (s b) -> p s b", s=CHUNK),
-                    op0=MULT,
-                    op1=ADD,
+        def multiply_slab(c, slab):
+            product = psum_mx.tile([P, BANK], F32, name="product")
+            for g in range(PASSES):
+                nc.tensor.matmul_mx(
+                    out=product[:],
+                    lhsT=wy_codes[:, slab, g, :].bitcast(FP8X4),
+                    lhsT_scale=wy_scales[:, slab, g, :],
+                    rhs=x_codes[c][:, g, :].bitcast(FP8X4),
+                    rhs_scale=x_scales[c][:, g, :],
+                    start=(g == 0),
+                    stop=(g == PASSES - 1),
                 )
+            nc.vector.scalar_tensor_tensor(
+                out=sums[c][:, slab, :].rearrange("p (s b) -> p s b", s=CHUNK),
+                in0=x_grouped[c][:, slab // 4, 1 : CHUNK + 1, :, slab % 4],
+                scalar=wx[:, slab : slab + 1],
+                in1=product[:].rearrange("p (s b) -> p s b", s=CHUNK),
+                op0=MULT,
+                op1=ADD,
+            )
 
-            if i + 1 < N_CHUNKS:
-                quantise_chunk(i + 1)
-
-            res = res_pool.tile([P, CHUNK, D], F32, name="res")
+        def finish_step(c, s):
+            res = res_pool.tile([P, D], F32, name="res")
             for n in range(D // BANK):
                 cols = slice(BANK * n, BANK * (n + 1))
-                for s in range(CHUNK):
-                    bank = psum_back.tile([P, 4, P], F32, name="bank_back")
-                    for q in range(4):
-                        nc.tensor.transpose(bank[:, q, :], sums[:, 4 * n + q, P * s : P * (s + 1)], ident_f32[:])
-                    nc.vector.tensor_tensor(
-                        out=res[:, s, cols].rearrange("b (u p e) -> b u p e", u=2, e=2),
-                        in0=bank[:].rearrange("b (u e) p -> b u p e", e=2),
-                        in1=context[:, cols].rearrange("b (u p e) -> b u p e", u=2, e=2),
-                        op=ADD,
-                    )
-                    if s % 2 == 1:
-                        step = 2 * n + s // 2
-                        if CHUNK * (i + 2) + step < STEPS:
-                            transpose_step(i + 2, step)
-            nc.sync.dma_start(out=out[:, CHUNK * i : CHUNK * (i + 1), :], in_=res[:])
+                bank = psum_back.tile([P, 4, P], F32, name="bank_back")
+                for q in range(4):
+                    nc.tensor.transpose(bank[:, q, :], sums[c][:, 4 * n + q, P * s : P * (s + 1)], ident_f32[:])
+                nc.vector.tensor_tensor(
+                    out=res[:, cols].rearrange("b (u p e) -> b u p e", u=2, e=2),
+                    in0=bank[:].rearrange("b (u e) p -> b u p e", e=2),
+                    in1=context[:, cols].rearrange("b (u p e) -> b u p e", u=2, e=2),
+                    op=ADD,
+                )
+            nc.sync.dma_start(out=out[:, CHUNK * c + s, :], in_=res[:])
+
+        for i in range(N_CHUNKS + 1):
+            if CHUNK * (i + 3) < STEPS:
+                load_chunk(i + 3)
+            if i < N_CHUNKS:
+                sums[i] = sum_pool.tile([P, SLABS, BANK], F32, name="sums")
+            for k in range(CHUNK):
+                if i < N_CHUNKS:
+                    multiply_slab(i, 2 * k)
+                    multiply_slab(i, 2 * k + 1)
+                if i > 0:
+                    finish_step(i - 1, k)
+                if CHUNK * (i + 2) + k < STEPS:
+                    transpose_step(i + 2, k)
+                if k % 2 == 1 and i + 1 < N_CHUNKS:
+                    quantise_pass(i + 1, k // 2)

@@ -28,9 +28,7 @@ FLOPS = 2 * P * LAGS * D * D + 2 * P * P * D
 
 
 def regroup(copy, bank, grouped):
-    halves = bank.bitcast(BF16).rearrange("p (g u) (c e) -> p g c u e", u=2, e=2)
-    for g in range(PASSES):
-        copy(out=grouped[:, g].rearrange("p c (u e) -> p c u e", e=2), in_=halves[:, g])
+    copy(out=grouped.bitcast(F32), in_=bank.rearrange("p (g u) c -> p g c u", u=2))
 
 
 def tile_npchangetransitionprior_pa_t_kernel(tc, x, emb, Wg, bg, out):
@@ -42,7 +40,7 @@ def tile_npchangetransitionprior_pa_t_kernel(tc, x, emb, Wg, bg, out):
         xg_pool = ctx.enter_context(tc.tile_pool(name="xg_pool", bufs=3))
         xq_pool = ctx.enter_context(tc.tile_pool(name="xq_pool", bufs=2))
         sum_pool = ctx.enter_context(tc.tile_pool(name="sum_pool", bufs=2))
-        res_pool = ctx.enter_context(tc.tile_pool(name="res_pool", bufs=4))
+        res_pool = ctx.enter_context(tc.tile_pool(name="res_pool", bufs=6))
         psum_in = ctx.enter_context(tc.psum_pool(name="psum_in", bufs=2))
         psum_mx = ctx.enter_context(tc.psum_pool(name="psum_mx", bufs=3))
         psum_back = ctx.enter_context(tc.psum_pool(name="psum_back", bufs=3))
@@ -129,26 +127,28 @@ def tile_npchangetransitionprior_pa_t_kernel(tc, x, emb, Wg, bg, out):
         for g in range(PASSES):
             quantise_pass(0, g)
 
-        emb_t_ps = psum_back.tile([P, P], BF16, name="emb_t_ps", tag="bank_back")
-        nc.tensor.transpose(emb_t_ps[:], emb_rows[:], ident_bf16[:])
-        emb_t = const.tile([P, P], BF16, name="emb_t")
-        nc.scalar.copy(out=emb_t[:], in_=emb_t_ps[:])
-        we_t_ps = psum_back.tile([P, SLABS, P], BF16, name="we_t_ps", tag="bank_back")
-        for w in range(WORD_BLOCKS):
-            for e in range(2):
-                nc.tensor.transpose(we_t_ps[:, 2 * w + e, :], wg[:, w, e, 0:P], ident_bf16[:])
-        we_t = const.tile([P, D], BF16, name="we_t")
-        nc.scalar.copy(
-            out=we_t[:].rearrange("h (w p e) -> h w p e", p=P, e=2),
-            in_=we_t_ps[:].rearrange("h (w e) p -> h w p e", e=2),
-        )
         context = const.tile([P, D], F32, name="context")
-        for n in range(D // BANK):
-            cols = slice(BANK * n, BANK * (n + 1))
-            context_ps = psum_mx.tile([P, BANK], F32, name="context_ps", tag="product")
-            nc.tensor.matmul(context_ps[:], lhsT=emb_t[:], rhs=we_t[:, cols], start=True, stop=False)
-            nc.tensor.matmul(context_ps[:], lhsT=ones[:], rhs=bias_row[:, cols], start=False, stop=True)
-            nc.scalar.copy(out=context[:, cols], in_=context_ps[:])
+
+        def make_context():
+            emb_t_ps = psum_back.tile([P, P], BF16, name="emb_t_ps", tag="bank_back")
+            nc.tensor.transpose(emb_t_ps[:], emb_rows[:], ident_bf16[:])
+            emb_t = const.tile([P, P], BF16, name="emb_t")
+            nc.scalar.copy(out=emb_t[:], in_=emb_t_ps[:])
+            we_t_ps = psum_back.tile([P, SLABS, P], BF16, name="we_t_ps", tag="bank_back")
+            for w in range(WORD_BLOCKS):
+                for e in range(2):
+                    nc.tensor.transpose(we_t_ps[:, 2 * w + e, :], wg[:, w, e, 0:P], ident_bf16[:])
+            we_t = const.tile([P, D], BF16, name="we_t")
+            nc.scalar.copy(
+                out=we_t[:].rearrange("h (w p e) -> h w p e", p=P, e=2),
+                in_=we_t_ps[:].rearrange("h (w e) p -> h w p e", e=2),
+            )
+            for n in range(D // BANK):
+                cols = slice(BANK * n, BANK * (n + 1))
+                context_ps = psum_mx.tile([P, BANK], F32, name="context_ps", tag="product")
+                nc.tensor.matmul(context_ps[:], lhsT=emb_t[:], rhs=we_t[:, cols], start=True, stop=False)
+                nc.tensor.matmul(context_ps[:], lhsT=ones[:], rhs=bias_row[:, cols], start=False, stop=True)
+                nc.scalar.copy(out=context[:, cols], in_=context_ps[:])
 
         def multiply_slab(c, slab):
             product = psum_mx.tile([P, BANK], F32, name="product")
@@ -178,12 +178,14 @@ def tile_npchangetransitionprior_pa_t_kernel(tc, x, emb, Wg, bg, out):
                 bank = psum_back.tile([P, 4, P], F32, name="bank_back")
                 for q in range(4):
                     nc.tensor.transpose(bank[:, q, :], sums[c][:, 4 * n + q, P * s : P * (s + 1)], ident_f32[:])
-                nc.vector.tensor_tensor(
-                    out=res[:, cols].rearrange("b (u p e) -> b u p e", u=2, e=2),
-                    in0=bank[:].rearrange("b (u e) p -> b u p e", e=2),
-                    in1=context[:, cols].rearrange("b (u p e) -> b u p e", u=2, e=2),
-                    op=ADD,
-                )
+                in_order = bank[:].rearrange("b (u e) p -> b u p e", e=2)
+                res_half = res[:, cols].rearrange("b (u p e) -> b u p e", u=2, e=2)
+                if n == 0:
+                    context_half = context[:, cols].rearrange("b (u p e) -> b u p e", u=2, e=2)
+                    nc.vector.tensor_tensor(out=res_half, in0=in_order, in1=context_half, op=ADD)
+                else:
+                    nc.scalar.copy(out=res_half, in_=in_order)
+                    nc.gpsimd.tensor_tensor(out=res[:, cols], in0=res[:, cols], in1=context[:, cols], op=ADD)
             nc.sync.dma_start(out=out[:, CHUNK * c + s, :], in_=res[:])
 
         for i in range(N_CHUNKS + 1):
@@ -201,3 +203,5 @@ def tile_npchangetransitionprior_pa_t_kernel(tc, x, emb, Wg, bg, out):
                     transpose_step(i + 2, k)
                 if k % 2 == 1 and i + 1 < N_CHUNKS:
                     quantise_pass(i + 1, k // 2)
+            if i == 0:
+                make_context()

@@ -22,7 +22,11 @@ WORD_BLOCKS = 4
 SLABS = 8
 CHUNK = 4
 N_CHUNKS = LAGS // CHUNK
+RUN_STEPS = 2
+RUNS = CHUNK // RUN_STEPS
 BANK = 512
+
+assert RUNS == PASSES
 
 FLOPS = 2 * P * LAGS * D * D + 2 * P * P * D
 
@@ -58,11 +62,11 @@ def tile_npchangetransitionprior_pa_t_kernel(tc, x, emb, Wg, bg, out):
             x_rows[c] = rows
 
         load_chunk(0)
+        load_chunk(1)
         wg = const.tile([P, WORD_BLOCKS, 2, ROW_PAD], BF16, name="wg")
         wg_rows = Wg.rearrange("(w p e) c -> w p e c", p=P, e=2)
         for w in range(WORD_BLOCKS):
             nc.sync.dma_start(out=wg[:, w, :, 0:ROW], in_=wg_rows[w])
-        load_chunk(1)
         load_chunk(2)
         emb_rows = const.tile([P, P], BF16, name="emb_rows")
         nc.scalar.dma_start(out=emb_rows[:], in_=emb)
@@ -98,15 +102,14 @@ def tile_npchangetransitionprior_pa_t_kernel(tc, x, emb, Wg, bg, out):
                 in_=x_grouped[c][:, g, 0:CHUNK, :, :].rearrange("p s b v -> p (s b v)"),
             )
 
-        for s in range(CHUNK):
-            transpose_step(0, s)
-
         wg_words = wg[:].bitcast(F32)
         wy_word0 = P // 2
         wy_grouped = const.tile([P, SLABS, PASSES, P, 4], BF16, name="wy_grouped", align_bytes=64)
         wy_codes = const.tile([P, SLABS, PASSES, P], U32, name="wy_codes", align_bytes=64)
         wy_scales = const.tile([P, SLABS, PASSES, P], U8, name="wy_scales", align_bytes=64)
-        for w in range(WORD_BLOCKS):
+        wx = const.tile([P, SLABS], F32, name="wx")
+
+        def prepare_slabs(w):
             for e in range(2):
                 bank = psum_in.tile([P, WORD_BLOCKS, P], F32, name="bank_in")
                 for k in range(WORD_BLOCKS):
@@ -114,18 +117,13 @@ def tile_npchangetransitionprior_pa_t_kernel(tc, x, emb, Wg, bg, out):
                     nc.tensor.transpose(bank[:, k, :], wg_words[:, w, e, first : first + P], ident_f32[:])
                 copy = nc.vector.tensor_copy if e == 0 else nc.scalar.copy
                 regroup(copy, bank[:], wy_grouped[:, 2 * w + e])
+            pair = slice(2 * w, 2 * w + 2)
             nc.vector.quantize_mx(
-                out=wy_codes[:, 2 * w : 2 * w + 2].rearrange("p l g m -> p (l g m)").bitcast(FP8X4),
-                scales=wy_scales[:, 2 * w : 2 * w + 2].rearrange("p l g m -> p (l g m)"),
-                in_=wy_grouped[:, 2 * w : 2 * w + 2].rearrange("p l g m v -> p (l g m v)"),
+                out=wy_codes[:, pair].rearrange("p l g m -> p (l g m)").bitcast(FP8X4),
+                scales=wy_scales[:, pair].rearrange("p l g m -> p (l g m)"),
+                in_=wy_grouped[:, pair].rearrange("p l g m v -> p (l g m v)"),
             )
-        wx = const.tile([P, SLABS], F32, name="wx")
-        nc.vector.tensor_copy(out=wx[:].rearrange("p (w e) -> p w e", e=2), in_=wg[:, :, :, ROW - 1])
-
-        for s in range(CHUNK):
-            transpose_step(1, s)
-        for g in range(PASSES):
-            quantise_pass(0, g)
+            nc.vector.tensor_copy(out=wx[:, pair], in_=wg[:, w, :, ROW - 1])
 
         context = const.tile([P, D], F32, name="context")
 
@@ -171,7 +169,7 @@ def tile_npchangetransitionprior_pa_t_kernel(tc, x, emb, Wg, bg, out):
                 op1=ADD,
             )
 
-        def finish_step(c, s):
+        def finish_step(c, s, vector_is_free):
             res = res_pool.tile([P, D], F32, name="res")
             for n in range(D // BANK):
                 cols = slice(BANK * n, BANK * (n + 1))
@@ -180,7 +178,7 @@ def tile_npchangetransitionprior_pa_t_kernel(tc, x, emb, Wg, bg, out):
                     nc.tensor.transpose(bank[:, q, :], sums[c][:, 4 * n + q, P * s : P * (s + 1)], ident_f32[:])
                 in_order = bank[:].rearrange("b (u e) p -> b u p e", e=2)
                 res_half = res[:, cols].rearrange("b (u p e) -> b u p e", u=2, e=2)
-                if n == 0:
+                if n == 1 and (s % RUN_STEPS == RUN_STEPS - 1 or vector_is_free):
                     context_half = context[:, cols].rearrange("b (u p e) -> b u p e", u=2, e=2)
                     nc.vector.tensor_tensor(out=res_half, in0=in_order, in1=context_half, op=ADD)
                 else:
@@ -188,20 +186,34 @@ def tile_npchangetransitionprior_pa_t_kernel(tc, x, emb, Wg, bg, out):
                     nc.gpsimd.tensor_tensor(out=res[:, cols], in0=res[:, cols], in1=context[:, cols], op=ADD)
             nc.sync.dma_start(out=out[:, CHUNK * c + s, :], in_=res[:])
 
+        for c in range(2):
+            for s in range(CHUNK):
+                transpose_step(c, s)
+        for g in range(PASSES):
+            quantise_pass(0, g)
+
+        slabs_a_run = SLABS // RUNS
         for i in range(N_CHUNKS + 1):
             if CHUNK * (i + 3) < STEPS:
                 load_chunk(i + 3)
             if i < N_CHUNKS:
                 sums[i] = sum_pool.tile([P, SLABS, BANK], F32, name="sums")
-            for k in range(CHUNK):
+            for r in range(RUNS):
+                run_steps = range(RUN_STEPS * r, RUN_STEPS * (r + 1))
+                run_slabs = range(slabs_a_run * r, slabs_a_run * (r + 1))
+                if i == 0:
+                    for w in range(run_slabs[0] // 2, run_slabs[-1] // 2 + 1):
+                        prepare_slabs(w)
                 if i < N_CHUNKS:
-                    multiply_slab(i, 2 * k)
-                    multiply_slab(i, 2 * k + 1)
+                    for slab in run_slabs:
+                        multiply_slab(i, slab)
                 if i > 0:
-                    finish_step(i - 1, k)
-                if CHUNK * (i + 2) + k < STEPS:
-                    transpose_step(i + 2, k)
-                if k % 2 == 1 and i + 1 < N_CHUNKS:
-                    quantise_pass(i + 1, k // 2)
+                    for s in run_steps:
+                        finish_step(i - 1, s, vector_is_free=(i == N_CHUNKS))
+                for s in run_steps:
+                    if CHUNK * (i + 2) + s < STEPS:
+                        transpose_step(i + 2, s)
+                if i + 1 < N_CHUNKS:
+                    quantise_pass(i + 1, r)
             if i == 0:
                 make_context()

@@ -22,11 +22,8 @@ WORD_BLOCKS = 4
 SLABS = 8
 CHUNK = 4
 N_CHUNKS = LAGS // CHUNK
-RUN_STEPS = 2
-RUNS = CHUNK // RUN_STEPS
+LEAD = 6
 BANK = 512
-
-assert RUNS == PASSES
 
 FLOPS = 2 * P * LAGS * D * D + 2 * P * P * D
 
@@ -178,7 +175,7 @@ def tile_npchangetransitionprior_pa_t_kernel(tc, x, emb, Wg, bg, out):
                     nc.tensor.transpose(bank[:, q, :], sums[c][:, 4 * n + q, P * s : P * (s + 1)], ident_f32[:])
                 in_order = bank[:].rearrange("b (u e) p -> b u p e", e=2)
                 res_half = res[:, cols].rearrange("b (u p e) -> b u p e", u=2, e=2)
-                if n == 1 and (s % RUN_STEPS == RUN_STEPS - 1 or vector_is_free):
+                if n == 0 or vector_is_free:
                     context_half = context[:, cols].rearrange("b (u p e) -> b u p e", u=2, e=2)
                     nc.vector.tensor_tensor(out=res_half, in0=in_order, in1=context_half, op=ADD)
                 else:
@@ -186,34 +183,27 @@ def tile_npchangetransitionprior_pa_t_kernel(tc, x, emb, Wg, bg, out):
                     nc.gpsimd.tensor_tensor(out=res[:, cols], in0=res[:, cols], in1=context[:, cols], op=ADD)
             nc.sync.dma_start(out=out[:, CHUNK * c + s, :], in_=res[:])
 
-        for c in range(2):
-            for s in range(CHUNK):
-                transpose_step(c, s)
+        for step in range(LEAD):
+            transpose_step(step // CHUNK, step % CHUNK)
         for g in range(PASSES):
             quantise_pass(0, g)
-
-        slabs_a_run = SLABS // RUNS
         for i in range(N_CHUNKS + 1):
             if CHUNK * (i + 3) < STEPS:
                 load_chunk(i + 3)
             if i < N_CHUNKS:
                 sums[i] = sum_pool.tile([P, SLABS, BANK], F32, name="sums")
-            for r in range(RUNS):
-                run_steps = range(RUN_STEPS * r, RUN_STEPS * (r + 1))
-                run_slabs = range(slabs_a_run * r, slabs_a_run * (r + 1))
+            for k in range(CHUNK):
+                if k >= CHUNK - PASSES and i + 1 < N_CHUNKS:
+                    quantise_pass(i + 1, k - (CHUNK - PASSES))
                 if i == 0:
-                    for w in range(run_slabs[0] // 2, run_slabs[-1] // 2 + 1):
-                        prepare_slabs(w)
+                    prepare_slabs(k)
                 if i < N_CHUNKS:
-                    for slab in run_slabs:
-                        multiply_slab(i, slab)
+                    multiply_slab(i, 2 * k)
+                    multiply_slab(i, 2 * k + 1)
                 if i > 0:
-                    for s in run_steps:
-                        finish_step(i - 1, s, vector_is_free=(i == N_CHUNKS))
-                for s in run_steps:
-                    if CHUNK * (i + 2) + s < STEPS:
-                        transpose_step(i + 2, s)
-                if i + 1 < N_CHUNKS:
-                    quantise_pass(i + 1, r)
+                    finish_step(i - 1, k, vector_is_free=(i == N_CHUNKS))
+                step = CHUNK * i + k + LEAD
+                if step < STEPS:
+                    transpose_step(step // CHUNK, step % CHUNK)
             if i == 0:
                 make_context()

from contextlib import ExitStack

import concourse.mybir as mybir
from concourse.masks import make_identity

F32 = mybir.dt.float32
BF16 = mybir.dt.bfloat16
U32 = mybir.dt.uint32
U8 = mybir.dt.uint8
FP8X4 = mybir.dt.float8_e4m3fn_x4
ADD = mybir.AluOpType.add
MULT = mybir.AluOpType.mult

P = 128
STEPS = 41
LAGS = STEPS - 1
D = 1024
ROW = P + D + 1
ROW_PAD = 1168
PASSES = 2
WORD_BLOCKS = 4
SLABS = 8
CHUNK = 4
N_CHUNKS = LAGS // CHUNK
LEAD = 6
BANK = 512

FLOPS = 2 * P * LAGS * D * D + 2 * P * P * D


def regroup(copy, bank, grouped):
    copy(out=grouped.bitcast(F32), in_=bank.rearrange("p (g u) c -> p g c u", u=2))


def tile_npchangetransitionprior_pa_t_kernel(tc, x, emb, Wg, bg, out):
    nc = tc.nc
    with ExitStack() as ctx:
        ctx.enter_context(tc.manual_schedule())
        const = ctx.enter_context(tc.tile_pool(name="const", bufs=1))
        xs_pool = ctx.enter_context(tc.tile_pool(name="xs_pool", bufs=3))
        xg_pool = ctx.enter_context(tc.tile_pool(name="xg_pool", bufs=3))
        xq_pool = ctx.enter_context(tc.tile_pool(name="xq_pool", bufs=2))
        sum_pool = ctx.enter_context(tc.tile_pool(name="sum_pool", bufs=2))
        res_pool = ctx.enter_context(tc.tile_pool(name="res_pool", bufs=6))
        psum_in = ctx.enter_context(tc.psum_pool(name="psum_in", bufs=2))
        psum_mx = ctx.enter_context(tc.psum_pool(name="psum_mx", bufs=3))
        psum_back = ctx.enter_context(tc.psum_pool(name="psum_back", bufs=3))

        x_rows = {}
        x_grouped = {}
        x_codes = {}
        x_scales = {}
        sums = {}

        def load_chunk(c):
            n_steps = min(CHUNK, STEPS - CHUNK * c)
            rows = xs_pool.tile([P, CHUNK, D], BF16, name="rows")
            nc.sync.dma_start(out=rows[:, 0:n_steps, :], in_=x[:, CHUNK * c : CHUNK * c + n_steps, :])
            x_rows[c] = rows

        load_chunk(0)
        load_chunk(1)
        wg = const.tile([P, WORD_BLOCKS, 2, ROW_PAD], BF16, name="wg")
        wg_rows = Wg.rearrange("(w p e) c -> w p e c", p=P, e=2)
        for w in range(WORD_BLOCKS):
            nc.sync.dma_start(out=wg[:, w, :, 0:ROW], in_=wg_rows[w])
        load_chunk(2)
        emb_rows = const.tile([P, P], BF16, name="emb_rows")
        nc.scalar.dma_start(out=emb_rows[:], in_=emb)
        bias_row = const.tile([P, D], BF16, name="bias_row")
        nc.vector.memset(bias_row[:], 0.0)
        nc.scalar.dma_start(out=bias_row[0:1, :], in_=bg.rearrange("(o d) -> o d", o=1))
        ones = const.tile([P, P], BF16, name="ones")
        nc.vector.memset(ones[:], 1.0)
        ident_f32 = const.tile([P, P], F32, name="ident_f32")
        make_identity(nc, ident_f32[:])
        ident_bf16 = const.tile([P, P], BF16, name="ident_bf16")
        make_identity(nc, ident_bf16[:])

        def transpose_step(c, s):
            words = x_rows[c][:].bitcast(F32)
            bank = psum_in.tile([P, WORD_BLOCKS, P], F32, name="bank_in")
            for w in range(WORD_BLOCKS):
                nc.tensor.transpose(bank[:, w, :], words[:, s, P * w : P * (w + 1)], ident_f32[:])
            if c < N_CHUNKS:
                if s == 0:
                    x_grouped[c] = xg_pool.tile([P, PASSES, CHUNK + 1, P, 4], BF16, name="grouped", align_bytes=64)
                regroup(nc.scalar.copy, bank[:], x_grouped[c][:, :, s, :, :])
            if s == 0 and c > 0:
                regroup(nc.scalar.copy, bank[:], x_grouped[c - 1][:, :, CHUNK, :, :])

        def quantise_pass(c, g):
            if g == 0:
                x_codes[c] = xq_pool.tile([P, PASSES, BANK], U32, name="codes", align_bytes=64)
                x_scales[c] = xq_pool.tile([P, PASSES, BANK], U8, name="scales", align_bytes=64)
            nc.vector.quantize_mx(
                out=x_codes[c][:, g, :].bitcast(FP8X4),
                scales=x_scales[c][:, g, :],
                in_=x_grouped[c][:, g, 0:CHUNK, :, :].rearrange("p s b v -> p (s b v)"),
            )

        wg_words = wg[:].bitcast(F32)
        wy_word0 = P // 2
        wy_grouped = const.tile([P, SLABS, PASSES, P, 4], BF16, name="wy_grouped", align_bytes=64)
        wy_codes = const.tile([P, SLABS, PASSES, P], U32, name="wy_codes", align_bytes=64)
        wy_scales = const.tile([P, SLABS, PASSES, P], U8, name="wy_scales", align_bytes=64)
        wx = const.tile([P, SLABS], F32, name="wx")

        def prepare_slabs(w):
            for e in range(2):
                bank = psum_in.tile([P, WORD_BLOCKS, P], F32, name="bank_in")
                for k in range(WORD_BLOCKS):
                    first = wy_word0 + P * k
                    nc.tensor.transpose(bank[:, k, :], wg_words[:, w, e, first : first + P], ident_f32[:])
                copy = nc.vector.tensor_copy if e == 0 else nc.scalar.copy
                regroup(copy, bank[:], wy_grouped[:, 2 * w + e])
            pair = slice(2 * w, 2 * w + 2)
            nc.vector.quantize_mx(
                out=wy_codes[:, pair].rearrange("p l g m -> p (l g m)").bitcast(FP8X4),
                scales=wy_scales[:, pair].rearrange("p l g m -> p (l g m)"),
                in_=wy_grouped[:, pair].rearrange("p l g m v -> p (l g m v)"),
            )
            nc.vector.tensor_copy(out=wx[:, pair], in_=wg[:, w, :, ROW - 1])

        context = const.tile([P, D], F32, name="context")

        def make_context():
            emb_t_ps = psum_back.tile([P, P], BF16, name="emb_t_ps", tag="bank_back")
            nc.tensor.transpose(emb_t_ps[:], emb_rows[:], ident_bf16[:])
            emb_t = const.tile([P, P], BF16, name="emb_t")
            nc.scalar.copy(out=emb_t[:], in_=emb_t_ps[:])
            we_t_ps = psum_back.tile([P, SLABS, P], BF16, name="we_t_ps", tag="bank_back")
            for w in range(WORD_BLOCKS):
                for e in range(2):
                    nc.tensor.transpose(we_t_ps[:, 2 * w + e, :], wg[:, w, e, 0:P], ident_bf16[:])
            we_t = const.tile([P, D], BF16, name="we_t")
            nc.scalar.copy(
                out=we_t[:].rearrange("h (w p e) -> h w p e", p=P, e=2),
                in_=we_t_ps[:].rearrange("h (w e) p -> h w p e", e=2),
            )
            for n in range(D // BANK):
                cols = slice(BANK * n, BANK * (n + 1))
                context_ps = psum_mx.tile([P, BANK], F32, name="context_ps", tag="product")
                nc.tensor.matmul(context_ps[:], lhsT=emb_t[:], rhs=we_t[:, cols], start=True, stop=False)
                nc.tensor.matmul(context_ps[:], lhsT=ones[:], rhs=bias_row[:, cols], start=False, stop=True)
                nc.scalar.copy(out=context[:, cols], in_=context_ps[:])

        def multiply_slab(c, slab):
            product = psum_mx.tile([P, BANK], F32, name="product")
            for g in range(PASSES):
                nc.tensor.matmul_mx(
                    out=product[:],
                    lhsT=wy_codes[:, slab, g, :].bitcast(FP8X4),
                    lhsT_scale=wy_scales[:, slab, g, :],
                    rhs=x_codes[c][:, g, :].bitcast(FP8X4),
                    rhs_scale=x_scales[c][:, g, :],
                    start=(g == 0),
                    stop=(g == PASSES - 1),
                )
            nc.vector.scalar_tensor_tensor(
                out=sums[c][:, slab, :].rearrange("p (s b) -> p s b", s=CHUNK),
                in0=x_grouped[c][:, slab // 4, 1 : CHUNK + 1, :, slab % 4],
                scalar=wx[:, slab : slab + 1],
                in1=product[:].rearrange("p (s b) -> p s b", s=CHUNK),
                op0=MULT,
                op1=ADD,
            )

        def finish_step(c, s, vector_is_free):
            res = res_pool.tile([P, D], F32, name="res")
            for n in range(D // BANK):
                cols = slice(BANK * n, BANK * (n + 1))
                bank = psum_back.tile([P, 4, P], F32, name="bank_back")
                for q in range(4):
                    nc.tensor.transpose(bank[:, q, :], sums[c][:, 4 * n + q, P * s : P * (s + 1)], ident_f32[:])
                in_order = bank[:].rearrange("b (u e) p -> b u p e", e=2)
                res_half = res[:, cols].rearrange("b (u p e) -> b u p e", u=2, e=2)
                if n == 0 or vector_is_free:
                    context_half = context[:, cols].rearrange("b (u p e) -> b u p e", u=2, e=2)
                    nc.vector.tensor_tensor(out=res_half, in0=in_order, in1=context_half, op=ADD)
                else:
                    nc.scalar.copy(out=res_half, in_=in_order)
                    nc.gpsimd.tensor_tensor(out=res[:, cols], in0=res[:, cols], in1=context[:, cols], op=ADD)
            nc.sync.dma_start(out=out[:, CHUNK * c + s, :], in_=res[:])

        for step in range(LEAD):
            transpose_step(step // CHUNK, step % CHUNK)
        for g in range(PASSES):
            quantise_pass(0, g)
        for i in range(N_CHUNKS + 1):
            if CHUNK * (i + 3) < STEPS:
                load_chunk(i + 3)
            if i < N_CHUNKS:
                sums[i] = sum_pool.tile([P, SLABS, BANK], F32, name="sums")
            for k in range(CHUNK):
                if k >= CHUNK - PASSES and i + 1 < N_CHUNKS:
                    quantise_pass(i + 1, k - (CHUNK - PASSES))
                if i == 0:
                    prepare_slabs(k)
                if i < N_CHUNKS:
                    multiply_slab(i, 2 * k)
                    multiply_slab(i, 2 * k + 1)
                if i > 0:
                    finish_step(i - 1, k, vector_is_free=(i == N_CHUNKS))
                step = CHUNK * i + k + LEAD
                if step < STEPS:
                    transpose_step(step // CHUNK, step % CHUNK)
            if i == 0:
                make_context()
